import numpy as np
import ml_dtypes


def mxq(x, axis, fmt="e4m3"):
    dtype, down = {"e4m3": (ml_dtypes.float8_e4m3fn, 7), "e5m2": (ml_dtypes.float8_e5m2, 14)}[fmt]
    v = np.moveaxis(np.asarray(x, np.float32).astype(ml_dtypes.bfloat16).astype(np.float64), axis, -1)
    blocks = v.reshape(v.shape[:-1] + (-1, 32))
    amax = np.abs(blocks).max(-1, keepdims=True)
    byte = np.maximum(np.where(amax > 0, np.frexp(amax)[1] - 1 + 127, 0) - down, 1)
    scale = np.exp2(byte - 127.0)
    codes = (blocks / scale).astype(np.float32).astype(dtype).astype(np.float64)
    return np.moveaxis((codes * scale).reshape(v.shape), -1, axis)


WIDE = False


def mx_kscale(k):
    if not WIDE:
        return np.ones(k)
    levels = np.array([10, -10, 5, -5, 0])
    a = np.random.permutation(np.resize(levels, k // 512 * 4)).reshape(k // 512, 4)
    idx = np.arange(k)
    return np.exp2(a[idx // 512, idx % 128 // 32])


BF16 = ml_dtypes.bfloat16


def bf(x):
    return np.asarray(x, np.float32).astype(BF16)


def f64(x):
    return np.asarray(x).astype(np.float64)


N, IN_DIM, HID, OUT_DIM = 1024, 1024, 512, 256


def setup_inputs():
    s = mx_kscale(IN_DIM)
    return {"X": bf(np.random.standard_normal((N, IN_DIM)) * s),
            "A": bf(np.random.uniform(0.0, 1.0, (N, N)) * 0.5 / np.sqrt(N)),
            "W_in": bf(np.random.standard_normal((IN_DIM, HID)) / np.sqrt(IN_DIM) / s[:, None]),
            "b_in": bf(np.random.standard_normal(HID) * 0.1),
            "eps0": bf(np.random.uniform(0.2, 0.4, (1,)))}


def reference(X, A, W_in, b_in, eps0):
    h = (mxq(f64(X), 1, "e4m3") @ mxq(f64(W_in), 0, "e4m3")) + f64(b_in)
    return (mxq(f64(A), 1, "e4m3") @ mxq(h, 0, "e4m3")) + (1.0 + f64(eps0)) * h

@@ -1,0 +1,186 @@
+from contextlib import ExitStack
+
+import concourse.mybir as mybir
+from concourse.masks import make_identity
+
+F32 = mybir.dt.float32
+BF16 = mybir.dt.bfloat16
+U32 = mybir.dt.uint32
+U8 = mybir.dt.uint8
+FP8X4 = mybir.dt.float8_e4m3fn_x4
+ADD = mybir.AluOpType.add
+MULT = mybir.AluOpType.mult
+
+P = 128
+NODES = 1024
+IN_DIM = 1024
+HID = 512
+K_PASS = 4 * P
+PASSES = 2
+PAIRS = NODES // (2 * P)
+F_CHUNKS = HID // P
+W_VECTOR_COLS = 2 * HID // 3 // 8 * 8
+
+FLOPS = 2 * NODES * IN_DIM * HID + 2 * NODES * NODES * HID
+
+
+def transpose_and_quantise(nc, psum, stage, identity, rows, codes, scales):
+    words = rows.bitcast(F32)
+    grouped = stage.tile([P, 2 * IN_DIM], BF16, tag="grouped", align_bytes=64)
+    grouped_words = grouped[:].bitcast(F32)
+    for e in range(2):
+        bank = psum.tile([P, 4, P], F32, tag="bank")
+        for gu in range(4):
+            first = e * (IN_DIM // 2) + gu * P
+            nc.tensor.transpose(bank[:, gu, :], words[:, first : first + P], identity)
+        nc.scalar.copy(
+            out=grouped_words[:, e * 512 : (e + 1) * 512].rearrange("p (g r u) -> p g r u", g=2, u=2),
+            in_=bank[:].rearrange("p (g u) r -> p g r u", u=2),
+        )
+    nc.vector.quantize_mx(out=codes.bitcast(FP8X4), scales=scales, in_=grouped[:])
+
+
+def tile_gin_pa_kernel(tc, X, A, W_in, b_in, eps0, out):
+    nc = tc.nc
+    x_view = X.rearrange("(c p e) k -> c p (e k)", p=P, e=2)
+    a_view = A.rearrange("(c p e) m -> c p (e m)", p=P, e=2)
+    out_view = out.rearrange("(c p e) f -> c p e f", p=P, e=2)
+    w_view = W_in.rearrange("(g u p e) f -> g p u (e f)", g=PASSES, u=2, p=P)
+
+    with ExitStack() as ctx:
+        keep = ctx.enter_context(tc.tile_pool(name="keep", bufs=1))
+        stage = ctx.enter_context(tc.tile_pool(name="stage", bufs=4))
+        psum = ctx.enter_context(tc.psum_pool(name="psum", bufs=8))
+
+        ones = keep.tile([P, P], BF16, name="ones")
+        nc.vector.memset(ones[:], 1.0)
+        b_row = keep.tile([P, HID], BF16, name="b_row")
+        nc.vector.memset(b_row[:], 0.0)
+        nc.sync.dma_start(out=b_row[0:1, :], in_=b_in.rearrange("(o f) -> o f", o=1))
+        eps_bf = keep.tile([P, 1], BF16, name="eps_bf")
+        nc.sync.dma_start(out=eps_bf[:], in_=eps0.partition_broadcast(P))
+        x_rows = []
+        for c in range(PAIRS):
+            x_rows.append(keep.tile([P, 2 * IN_DIM], BF16, name="x_rows%d" % c))
+        nc.sync.dma_start(out=x_rows[0][:], in_=x_view[0])
+        w_raw = []
+        for g in range(PASSES):
+            w_rows = keep.tile([P, 4, HID], BF16, name="w_raw%d" % g)
+            nc.sync.dma_start(out=w_rows[:].rearrange("p (u e) f -> p u (e f)", u=2), in_=w_view[g])
+            w_raw.append(w_rows)
+        for c in range(1, PAIRS):
+            nc.sync.dma_start(out=x_rows[c][:], in_=x_view[c])
+        a_rows = []
+        for c in range(PAIRS):
+            rows = keep.tile([P, 2 * NODES], BF16, name="a_rows%d" % c)
+            nc.sync.dma_start(out=rows[:], in_=a_view[c])
+            a_rows.append(rows)
+
+        identity = keep.tile([P, P], F32, name="identity")
+        make_identity(nc, identity[:])
+        one_plus_eps = keep.tile([P, 1], F32, name="one_plus_eps")
+        nc.vector.tensor_scalar_add(out=one_plus_eps[:], in0=eps_bf[:], scalar1=1.0)
+        bias_bank = psum.tile([P, HID], F32, tag="bank")
+        nc.tensor.matmul(out=bias_bank[:], lhsT=ones[:], rhs=b_row[:], start=True, stop=True)
+        bias = keep.tile([P, HID], F32, name="bias")
+        nc.scalar.copy(out=bias[:], in_=bias_bank[:])
+
+        w_codes = []
+        w_scales = []
+        for g in range(PASSES):
+            w_grouped = keep.tile([P, 4 * HID], BF16, name="w_grouped%d" % g, align_bytes=64)
+            nc.vector.tensor_copy(
+                out=w_grouped[:, : 4 * W_VECTOR_COLS].rearrange("p (c i t) -> p c t i", i=4, t=4),
+                in_=w_raw[g][:, :, :W_VECTOR_COLS].rearrange("p t (c i) -> p c t i", i=4),
+            )
+            nc.scalar.copy(
+                out=w_grouped[:, 4 * W_VECTOR_COLS :].rearrange("p (c i t) -> p c t i", i=4, t=4),
+                in_=w_raw[g][:, :, W_VECTOR_COLS:].rearrange("p t (c i) -> p c t i", i=4),
+            )
+            codes = keep.tile([P, HID], U32, name="w_codes%d" % g, align_bytes=64)
+            scales = keep.tile([P, HID], U8, name="w_scales%d" % g, align_bytes=64)
+            nc.vector.quantize_mx(out=codes[:].bitcast(FP8X4), scales=scales[:], in_=w_grouped[:])
+            w_codes.append(codes)
+            w_scales.append(scales)
+
+        def quantise_rows(rows, name):
+            codes = keep.tile([P, 4 * P], U32, name=name + "_codes", align_bytes=64)
+            scales = keep.tile([P, 4 * P], U8, name=name + "_scales", align_bytes=64)
+            transpose_and_quantise(nc, psum, stage, identity[:], rows[:], codes[:], scales[:])
+            return codes, scales
+
+        h32 = []
+        h_codes = []
+        h_scales = []
+
+        def project(g, x_q):
+            h_f32 = keep.tile([P, HID, 4], F32, name="h32_%d" % g)
+            h_grouped = keep.tile([P, 4 * HID], BF16, name="h_grouped%d" % g, align_bytes=64)
+            codes_h = keep.tile([P, HID], U32, name="h_codes%d" % g, align_bytes=64)
+            scales_h = keep.tile([P, HID], U8, name="h_scales%d" % g, align_bytes=64)
+            for cf in range(F_CHUNKS):
+                f_cols = slice(cf * P, (cf + 1) * P)
+                bank = psum.tile([P, 4, P], F32, tag="bank")
+                for t in range(4):
+                    codes, scales = x_q[2 * g + t // 2]
+                    for kp in range(PASSES):
+                        first = ((t % 2) * PASSES + kp) * P
+                        nc.tensor.matmul_mx(
+                            out=bank[:, t, :],
+                            lhsT=codes[:, first : first + P].bitcast(FP8X4),
+                            lhsT_scale=scales[:, first : first + P],
+                            rhs=w_codes[kp][:, f_cols].bitcast(FP8X4),
+                            rhs_scale=w_scales[kp][:, f_cols],
+                            start=(kp == 0),
+                            stop=(kp == PASSES - 1),
+                        )
+                nc.vector.tensor_tensor(
+                    out=h_f32[:, f_cols, :],
+                    in0=bank[:].rearrange("p t f -> p f t"),
+                    in1=bias[:, f_cols].unsqueeze(2).to_broadcast([P, P, 4]),
+                    op=ADD,
+                )
+                nc.scalar.copy(
+                    out=h_grouped[:, cf * 4 * P : (cf + 1) * 4 * P],
+                    in_=h_f32[:, f_cols, :].rearrange("p f t -> p (f t)"),
+                )
+                nc.vector.quantize_mx(
+                    out=codes_h[:, f_cols].bitcast(FP8X4),
+                    scales=scales_h[:, f_cols],
+                    in_=h_grouped[:, cf * 4 * P : (cf + 1) * 4 * P],
+                )
+            h32.append(h_f32)
+            h_codes.append(codes_h)
+            h_scales.append(scales_h)
+
+        x_q = [quantise_rows(x_rows[c], "x%d" % c) for c in range(PAIRS)]
+        for g in range(PASSES):
+            project(g, x_q)
+
+        a_q = [quantise_rows(a_rows[c], "a%d" % c) for c in range(PAIRS)]
+
+        for c in range(PAIRS):
+            codes, scales = a_q[c]
+            for e in range(2):
+                acc = psum.tile([P, HID], F32, tag="bank")
+                for g in range(PASSES):
+                    first = (e * PASSES + g) * P
+                    nc.tensor.matmul_mx(
+                        out=acc[:],
+                        lhsT=codes[:, first : first + P].bitcast(FP8X4),
+                        lhsT_scale=scales[:, first : first + P],
+                        rhs=h_codes[g][:].bitcast(FP8X4),
+                        rhs_scale=h_scales[g][:],
+                        start=(g == 0),
+                        stop=(g == PASSES - 1),
+                    )
+                result = stage.tile([P, HID], F32, tag="result")
+                nc.vector.scalar_tensor_tensor(
+                    out=result[:],
+                    in0=h32[c // 2][:, :, 2 * (c % 2) + e],
+                    scalar=one_plus_eps[:, 0:1],
+                    in1=acc[:],
+                    op0=MULT,
+                    op1=ADD,
+                )
+                nc.sync.dma_start(out=out_view[c][:, e, :], in_=result[:])

@@ -24,7 +24,7 @@ W_VECTOR_COLS = 2 * HID // 3 // 8 * 8
 FLOPS = 2 * NODES * IN_DIM * HID + 2 * NODES * NODES * HID
 
 
-def transpose_and_quantise(nc, psum, stage, identity, rows, codes, scales):
+def transpose_rows(nc, psum, stage, identity, rows):
     words = rows.bitcast(F32)
     grouped = stage.tile([P, 2 * IN_DIM], BF16, tag="grouped", align_bytes=64)
     grouped_words = grouped[:].bitcast(F32)
@@ -37,7 +37,7 @@ def transpose_and_quantise(nc, psum, stage, identity, rows, codes, scales):
             out=grouped_words[:, e * 512 : (e + 1) * 512].rearrange("p (g r u) -> p g r u", g=2, u=2),
             in_=bank[:].rearrange("p (g u) r -> p g r u", u=2),
         )
-    nc.vector.quantize_mx(out=codes.bitcast(FP8X4), scales=scales, in_=grouped[:])
+    return grouped
 
 
 def tile_gin_pa_kernel(tc, X, A, W_in, b_in, eps0, out):
@@ -51,6 +51,7 @@ def tile_gin_pa_kernel(tc, X, A, W_in, b_in, eps0, out):
         keep = ctx.enter_context(tc.tile_pool(name="keep", bufs=1))
         stage = ctx.enter_context(tc.tile_pool(name="stage", bufs=4))
         psum = ctx.enter_context(tc.psum_pool(name="psum", bufs=8))
+        ctx.enter_context(tc.manual_schedule())
 
         ones = keep.tile([P, P], BF16, name="ones")
         nc.vector.memset(ones[:], 1.0)
@@ -78,16 +79,17 @@ def tile_gin_pa_kernel(tc, X, A, W_in, b_in, eps0, out):
 
         identity = keep.tile([P, P], F32, name="identity")
         make_identity(nc, identity[:])
-        one_plus_eps = keep.tile([P, 1], F32, name="one_plus_eps")
-        nc.vector.tensor_scalar_add(out=one_plus_eps[:], in0=eps_bf[:], scalar1=1.0)
-        bias_bank = psum.tile([P, HID], F32, tag="bank")
-        nc.tensor.matmul(out=bias_bank[:], lhsT=ones[:], rhs=b_row[:], start=True, stop=True)
-        bias = keep.tile([P, HID], F32, name="bias")
-        nc.scalar.copy(out=bias[:], in_=bias_bank[:])
 
-        w_codes = []
-        w_scales = []
-        for g in range(PASSES):
+        def transposed(rows):
+            return transpose_rows(nc, psum, stage, identity[:], rows[:])
+
+        def quantised(grouped, width, name):
+            codes = keep.tile([P, width], U32, name=name + "_codes", align_bytes=64)
+            scales = keep.tile([P, width], U8, name=name + "_scales", align_bytes=64)
+            nc.vector.quantize_mx(out=codes[:].bitcast(FP8X4), scales=scales[:], in_=grouped[:])
+            return codes, scales
+
+        def regroup_w(g):
             w_grouped = keep.tile([P, 4 * HID], BF16, name="w_grouped%d" % g, align_bytes=64)
             nc.vector.tensor_copy(
                 out=w_grouped[:, : 4 * W_VECTOR_COLS].rearrange("p (c i t) -> p c t i", i=4, t=4),
@@ -97,67 +99,72 @@ def tile_gin_pa_kernel(tc, X, A, W_in, b_in, eps0, out):
                 out=w_grouped[:, 4 * W_VECTOR_COLS :].rearrange("p (c i t) -> p c t i", i=4, t=4),
                 in_=w_raw[g][:, :, W_VECTOR_COLS:].rearrange("p t (c i) -> p c t i", i=4),
             )
-            codes = keep.tile([P, HID], U32, name="w_codes%d" % g, align_bytes=64)
-            scales = keep.tile([P, HID], U8, name="w_scales%d" % g, align_bytes=64)
-            nc.vector.quantize_mx(out=codes[:].bitcast(FP8X4), scales=scales[:], in_=w_grouped[:])
-            w_codes.append(codes)
-            w_scales.append(scales)
+            return w_grouped
 
-        def quantise_rows(rows, name):
-            codes = keep.tile([P, 4 * P], U32, name=name + "_codes", align_bytes=64)
-            scales = keep.tile([P, 4 * P], U8, name=name + "_scales", align_bytes=64)
-            transpose_and_quantise(nc, psum, stage, identity[:], rows[:], codes[:], scales[:])
-            return codes, scales
+        x_grouped = [transposed(x_rows[0])]
+        w_grouped0 = regroup_w(0)
+        x_q = [quantised(x_grouped[0], 4 * P, "x0")]
+        w_grouped1 = regroup_w(1)
+        w_q = [quantised(w_grouped0, HID, "w0"), quantised(w_grouped1, HID, "w1")]
 
-        h32 = []
-        h_codes = []
-        h_scales = []
+        bias_bank = psum.tile([P, HID], F32, tag="bank")
+        nc.tensor.matmul(out=bias_bank[:], lhsT=ones[:], rhs=b_row[:], start=True, stop=True)
+        bias = keep.tile([P, HID], F32, name="bias")
+        nc.scalar.copy(out=bias[:], in_=bias_bank[:])
+        one_plus_eps = keep.tile([P, 1], F32, name="one_plus_eps")
+        nc.vector.tensor_scalar_add(out=one_plus_eps[:], in0=eps_bf[:], scalar1=1.0)
 
-        def project(g, x_q):
-            h_f32 = keep.tile([P, HID, 4], F32, name="h32_%d" % g)
-            h_grouped = keep.tile([P, 4 * HID], BF16, name="h_grouped%d" % g, align_bytes=64)
-            codes_h = keep.tile([P, HID], U32, name="h_codes%d" % g, align_bytes=64)
-            scales_h = keep.tile([P, HID], U8, name="h_scales%d" % g, align_bytes=64)
-            for cf in range(F_CHUNKS):
-                f_cols = slice(cf * P, (cf + 1) * P)
-                bank = psum.tile([P, 4, P], F32, tag="bank")
-                for t in range(4):
-                    codes, scales = x_q[2 * g + t // 2]
-                    for kp in range(PASSES):
-                        first = ((t % 2) * PASSES + kp) * P
-                        nc.tensor.matmul_mx(
-                            out=bank[:, t, :],
-                            lhsT=codes[:, first : first + P].bitcast(FP8X4),
-                            lhsT_scale=scales[:, first : first + P],
-                            rhs=w_codes[kp][:, f_cols].bitcast(FP8X4),
-                            rhs_scale=w_scales[kp][:, f_cols],
-                            start=(kp == 0),
-                            stop=(kp == PASSES - 1),
-                        )
-                nc.vector.tensor_tensor(
-                    out=h_f32[:, f_cols, :],
-                    in0=bank[:].rearrange("p t f -> p f t"),
-                    in1=bias[:, f_cols].unsqueeze(2).to_broadcast([P, P, 4]),
-                    op=ADD,
-                )
-                nc.scalar.copy(
-                    out=h_grouped[:, cf * 4 * P : (cf + 1) * 4 * P],
-                    in_=h_f32[:, f_cols, :].rearrange("p f t -> p (f t)"),
-                )
-                nc.vector.quantize_mx(
-                    out=codes_h[:, f_cols].bitcast(FP8X4),
-                    scales=scales_h[:, f_cols],
-                    in_=h_grouped[:, cf * 4 * P : (cf + 1) * 4 * P],
-                )
-            h32.append(h_f32)
-            h_codes.append(codes_h)
-            h_scales.append(scales_h)
+        for c in range(1, PAIRS):
+            x_grouped.append(transposed(x_rows[c]))
+        for c in range(1, PAIRS):
+            x_q.append(quantised(x_grouped[c], 4 * P, "x%d" % c))
 
-        x_q = [quantise_rows(x_rows[c], "x%d" % c) for c in range(PAIRS)]
-        for g in range(PASSES):
-            project(g, x_q)
+        h32 = [keep.tile([P, HID, 4], F32, name="h32_%d" % g) for g in range(PASSES)]
+        h_grouped = [keep.tile([P, 4 * HID], BF16, name="h_grouped%d" % g, align_bytes=64) for g in range(PASSES)]
+        h_codes = [keep.tile([P, HID], U32, name="h_codes%d" % g, align_bytes=64) for g in range(PASSES)]
+        h_scales = [keep.tile([P, HID], U8, name="h_scales%d" % g, align_bytes=64) for g in range(PASSES)]
 
-        a_q = [quantise_rows(a_rows[c], "a%d" % c) for c in range(PAIRS)]
+        def quantise_h(g, cf):
+            nc.vector.quantize_mx(
+                out=h_codes[g][:, cf * P : (cf + 1) * P].bitcast(FP8X4),
+                scales=h_scales[g][:, cf * P : (cf + 1) * P],
+                in_=h_grouped[g][:, cf * 4 * P : (cf + 1) * 4 * P],
+            )
+
+        for i in range(PASSES * F_CHUNKS):
+            g, cf = i // F_CHUNKS, i % F_CHUNKS
+            f_cols = slice(cf * P, (cf + 1) * P)
+            bank = psum.tile([P, 4, P], F32, tag="bank")
+            for t in range(4):
+                codes, scales = x_q[2 * g + t // 2]
+                for kp in range(PASSES):
+                    first = ((t % 2) * PASSES + kp) * P
+                    nc.tensor.matmul_mx(
+                        out=bank[:, t, :],
+                        lhsT=codes[:, first : first + P].bitcast(FP8X4),
+                        lhsT_scale=scales[:, first : first + P],
+                        rhs=w_q[kp][0][:, f_cols].bitcast(FP8X4),
+                        rhs_scale=w_q[kp][1][:, f_cols],
+                        start=(kp == 0),
+                        stop=(kp == PASSES - 1),
+                    )
+            nc.vector.tensor_tensor(
+                out=h32[g][:, f_cols, :],
+                in0=bank[:].rearrange("p t f -> p f t"),
+                in1=bias[:, f_cols].unsqueeze(2).to_broadcast([P, P, 4]),
+                op=ADD,
+            )
+            nc.scalar.copy(
+                out=h_grouped[g][:, cf * 4 * P : (cf + 1) * 4 * P],
+                in_=h32[g][:, f_cols, :].rearrange("p f t -> p (f t)"),
+            )
+            if i > 0:
+                quantise_h((i - 1) // F_CHUNKS, (i - 1) % F_CHUNKS)
+
+        a_grouped = [transposed(a_rows[c]) for c in range(PAIRS)]
+        a_q = [quantised(a_grouped[0], 4 * P, "a0")]
+        quantise_h(PASSES - 1, F_CHUNKS - 1)
+        a_q.append(quantised(a_grouped[1], 4 * P, "a1"))
 
         for c in range(PAIRS):
             codes, scales = a_q[c]
@@ -184,3 +191,5 @@ def tile_gin_pa_kernel(tc, X, A, W_in, b_in, eps0, out):
                     op1=ADD,
                 )
                 nc.sync.dma_start(out=out_view[c][:, e, :], in_=result[:])
+            if c + 2 < PAIRS:
+                a_q.append(quantised(a_grouped[c + 2], 4 * P, "a%d" % (c + 2)))

@@ -24,7 +24,7 @@ W_VECTOR_COLS = 2 * HID // 3 // 8 * 8
 FLOPS = 2 * NODES * IN_DIM * HID + 2 * NODES * NODES * HID
 
 
-def transpose_rows(nc, psum, stage, identity, rows):
+def transpose_and_quantise(nc, psum, stage, identity, rows, codes, scales):
     words = rows.bitcast(F32)
     grouped = stage.tile([P, 2 * IN_DIM], BF16, tag="grouped", align_bytes=64)
     grouped_words = grouped[:].bitcast(F32)
@@ -37,7 +37,7 @@ def transpose_rows(nc, psum, stage, identity, rows):
             out=grouped_words[:, e * 512 : (e + 1) * 512].rearrange("p (g r u) -> p g r u", g=2, u=2),
             in_=bank[:].rearrange("p (g u) r -> p g r u", u=2),
         )
-    return grouped
+    nc.vector.quantize_mx(out=codes.bitcast(FP8X4), scales=scales, in_=grouped[:])
 
 
 def tile_gin_pa_kernel(tc, X, A, W_in, b_in, eps0, out):
@@ -51,7 +51,6 @@ def tile_gin_pa_kernel(tc, X, A, W_in, b_in, eps0, out):
         keep = ctx.enter_context(tc.tile_pool(name="keep", bufs=1))
         stage = ctx.enter_context(tc.tile_pool(name="stage", bufs=4))
         psum = ctx.enter_context(tc.psum_pool(name="psum", bufs=8))
-        ctx.enter_context(tc.manual_schedule())
 
         ones = keep.tile([P, P], BF16, name="ones")
         nc.vector.memset(ones[:], 1.0)
@@ -79,17 +78,16 @@ def tile_gin_pa_kernel(tc, X, A, W_in, b_in, eps0, out):
 
         identity = keep.tile([P, P], F32, name="identity")
         make_identity(nc, identity[:])
+        one_plus_eps = keep.tile([P, 1], F32, name="one_plus_eps")
+        nc.vector.tensor_scalar_add(out=one_plus_eps[:], in0=eps_bf[:], scalar1=1.0)
+        bias_bank = psum.tile([P, HID], F32, tag="bank")
+        nc.tensor.matmul(out=bias_bank[:], lhsT=ones[:], rhs=b_row[:], start=True, stop=True)
+        bias = keep.tile([P, HID], F32, name="bias")
+        nc.scalar.copy(out=bias[:], in_=bias_bank[:])
 
-        def transposed(rows):
-            return transpose_rows(nc, psum, stage, identity[:], rows[:])
-
-        def quantised(grouped, width, name):
-            codes = keep.tile([P, width], U32, name=name + "_codes", align_bytes=64)
-            scales = keep.tile([P, width], U8, name=name + "_scales", align_bytes=64)
-            nc.vector.quantize_mx(out=codes[:].bitcast(FP8X4), scales=scales[:], in_=grouped[:])
-            return codes, scales
-
-        def regroup_w(g):
+        w_codes = []
+        w_scales = []
+        for g in range(PASSES):
             w_grouped = keep.tile([P, 4 * HID], BF16, name="w_grouped%d" % g, align_bytes=64)
             nc.vector.tensor_copy(
                 out=w_grouped[:, : 4 * W_VECTOR_COLS].rearrange("p (c i t) -> p c t i", i=4, t=4),
@@ -99,72 +97,67 @@ def tile_gin_pa_kernel(tc, X, A, W_in, b_in, eps0, out):
                 out=w_grouped[:, 4 * W_VECTOR_COLS :].rearrange("p (c i t) -> p c t i", i=4, t=4),
                 in_=w_raw[g][:, :, W_VECTOR_COLS:].rearrange("p t (c i) -> p c t i", i=4),
             )
-            return w_grouped
+            codes = keep.tile([P, HID], U32, name="w_codes%d" % g, align_bytes=64)
+            scales = keep.tile([P, HID], U8, name="w_scales%d" % g, align_bytes=64)
+            nc.vector.quantize_mx(out=codes[:].bitcast(FP8X4), scales=scales[:], in_=w_grouped[:])
+            w_codes.append(codes)
+            w_scales.append(scales)
 
-        x_grouped = [transposed(x_rows[0])]
-        w_grouped0 = regroup_w(0)
-        x_q = [quantised(x_grouped[0], 4 * P, "x0")]
-        w_grouped1 = regroup_w(1)
-        w_q = [quantised(w_grouped0, HID, "w0"), quantised(w_grouped1, HID, "w1")]
+        def quantise_rows(rows, name):
+            codes = keep.tile([P, 4 * P], U32, name=name + "_codes", align_bytes=64)
+            scales = keep.tile([P, 4 * P], U8, name=name + "_scales", align_bytes=64)
+            transpose_and_quantise(nc, psum, stage, identity[:], rows[:], codes[:], scales[:])
+            return codes, scales
 
-        bias_bank = psum.tile([P, HID], F32, tag="bank")
-        nc.tensor.matmul(out=bias_bank[:], lhsT=ones[:], rhs=b_row[:], start=True, stop=True)
-        bias = keep.tile([P, HID], F32, name="bias")
-        nc.scalar.copy(out=bias[:], in_=bias_bank[:])
-        one_plus_eps = keep.tile([P, 1], F32, name="one_plus_eps")
-        nc.vector.tensor_scalar_add(out=one_plus_eps[:], in0=eps_bf[:], scalar1=1.0)
+        h32 = []
+        h_codes = []
+        h_scales = []
 
-        for c in range(1, PAIRS):
-            x_grouped.append(transposed(x_rows[c]))
-        for c in range(1, PAIRS):
-            x_q.append(quantised(x_grouped[c], 4 * P, "x%d" % c))
+        def project(g, x_q):
+            h_f32 = keep.tile([P, 4, HID], F32, name="h32_%d" % g)
+            h_grouped = keep.tile([P, 4 * HID], BF16, name="h_grouped%d" % g, align_bytes=64)
+            codes_h = keep.tile([P, HID], U32, name="h_codes%d" % g, align_bytes=64)
+            scales_h = keep.tile([P, HID], U8, name="h_scales%d" % g, align_bytes=64)
+            for cf in range(F_CHUNKS):
+                f_cols = slice(cf * P, (cf + 1) * P)
+                bank = psum.tile([P, 4, P], F32, tag="bank")
+                for t in range(4):
+                    codes, scales = x_q[2 * g + t // 2]
+                    for kp in range(PASSES):
+                        first = ((t % 2) * PASSES + kp) * P
+                        nc.tensor.matmul_mx(
+                            out=bank[:, t, :],
+                            lhsT=codes[:, first : first + P].bitcast(FP8X4),
+                            lhsT_scale=scales[:, first : first + P],
+                            rhs=w_codes[kp][:, f_cols].bitcast(FP8X4),
+                            rhs_scale=w_scales[kp][:, f_cols],
+                            start=(kp == 0),
+                            stop=(kp == PASSES - 1),
+                        )
+                nc.vector.tensor_tensor(
+                    out=h_f32[:, :, f_cols],
+                    in0=bank[:],
+                    in1=bias[:, f_cols].unsqueeze(1).to_broadcast([P, 4, P]),
+                    op=ADD,
+                )
+                nc.scalar.copy(
+                    out=h_grouped[:, cf * 4 * P : (cf + 1) * 4 * P].rearrange("p (f t) -> p f t", t=4),
+                    in_=h_f32[:, :, f_cols].rearrange("p t f -> p f t"),
+                )
+                nc.vector.quantize_mx(
+                    out=codes_h[:, f_cols].bitcast(FP8X4),
+                    scales=scales_h[:, f_cols],
+                    in_=h_grouped[:, cf * 4 * P : (cf + 1) * 4 * P],
+                )
+            h32.append(h_f32)
+            h_codes.append(codes_h)
+            h_scales.append(scales_h)
 
-        h32 = [keep.tile([P, HID, 4], F32, name="h32_%d" % g) for g in range(PASSES)]
-        h_grouped = [keep.tile([P, 4 * HID], BF16, name="h_grouped%d" % g, align_bytes=64) for g in range(PASSES)]
-        h_codes = [keep.tile([P, HID], U32, name="h_codes%d" % g, align_bytes=64) for g in range(PASSES)]
-        h_scales = [keep.tile([P, HID], U8, name="h_scales%d" % g, align_bytes=64) for g in range(PASSES)]
+        x_q = [quantise_rows(x_rows[c], "x%d" % c) for c in range(PAIRS)]
+        for g in range(PASSES):
+            project(g, x_q)
 
-        def quantise_h(g, cf):
-            nc.vector.quantize_mx(
-                out=h_codes[g][:, cf * P : (cf + 1) * P].bitcast(FP8X4),
-                scales=h_scales[g][:, cf * P : (cf + 1) * P],
-                in_=h_grouped[g][:, cf * 4 * P : (cf + 1) * 4 * P],
-            )
-
-        for i in range(PASSES * F_CHUNKS):
-            g, cf = i // F_CHUNKS, i % F_CHUNKS
-            f_cols = slice(cf * P, (cf + 1) * P)
-            bank = psum.tile([P, 4, P], F32, tag="bank")
-            for t in range(4):
-                codes, scales = x_q[2 * g + t // 2]
-                for kp in range(PASSES):
-                    first = ((t % 2) * PASSES + kp) * P
-                    nc.tensor.matmul_mx(
-                        out=bank[:, t, :],
-                        lhsT=codes[:, first : first + P].bitcast(FP8X4),
-                        lhsT_scale=scales[:, first : first + P],
-                        rhs=w_q[kp][0][:, f_cols].bitcast(FP8X4),
-                        rhs_scale=w_q[kp][1][:, f_cols],
-                        start=(kp == 0),
-                        stop=(kp == PASSES - 1),
-                    )
-            nc.vector.tensor_tensor(
-                out=h32[g][:, f_cols, :],
-                in0=bank[:].rearrange("p t f -> p f t"),
-                in1=bias[:, f_cols].unsqueeze(2).to_broadcast([P, P, 4]),
-                op=ADD,
-            )
-            nc.scalar.copy(
-                out=h_grouped[g][:, cf * 4 * P : (cf + 1) * 4 * P],
-                in_=h32[g][:, f_cols, :].rearrange("p f t -> p (f t)"),
-            )
-            if i > 0:
-                quantise_h((i - 1) // F_CHUNKS, (i - 1) % F_CHUNKS)
-
-        a_grouped = [transposed(a_rows[c]) for c in range(PAIRS)]
-        a_q = [quantised(a_grouped[0], 4 * P, "a0")]
-        quantise_h(PASSES - 1, F_CHUNKS - 1)
-        a_q.append(quantised(a_grouped[1], 4 * P, "a1"))
+        a_q = [quantise_rows(a_rows[c], "a%d" % c) for c in range(PAIRS)]
 
         for c in range(PAIRS):
             codes, scales = a_q[c]
@@ -184,12 +177,10 @@ def tile_gin_pa_kernel(tc, X, A, W_in, b_in, eps0, out):
                 result = stage.tile([P, HID], F32, tag="result")
                 nc.vector.scalar_tensor_tensor(
                     out=result[:],
-                    in0=h32[c // 2][:, :, 2 * (c % 2) + e],
+                    in0=h32[c // 2][:, 2 * (c % 2) + e, :],
                     scalar=one_plus_eps[:, 0:1],
                     in1=acc[:],
                     op0=MULT,
                     op1=ADD,
                 )
                 nc.sync.dma_start(out=out_view[c][:, e, :], in_=result[:])
-            if c + 2 < PAIRS:
-                a_q.append(quantised(a_grouped[c + 2], 4 * P, "a%d" % (c + 2)))

@@ -24,7 +24,7 @@ W_VECTOR_COLS = 2 * HID // 3 // 8 * 8
 FLOPS = 2 * NODES * IN_DIM * HID + 2 * NODES * NODES * HID
 
 
-def transpose_and_quantise(nc, psum, stage, identity, rows, codes, scales):
+def transpose_rows(nc, psum, stage, identity, rows):
     words = rows.bitcast(F32)
     grouped = stage.tile([P, 2 * IN_DIM], BF16, tag="grouped", align_bytes=64)
     grouped_words = grouped[:].bitcast(F32)
@@ -37,7 +37,7 @@ def transpose_and_quantise(nc, psum, stage, identity, rows, codes, scales):
             out=grouped_words[:, e * 512 : (e + 1) * 512].rearrange("p (g r u) -> p g r u", g=2, u=2),
             in_=bank[:].rearrange("p (g u) r -> p g r u", u=2),
         )
-    nc.vector.quantize_mx(out=codes.bitcast(FP8X4), scales=scales, in_=grouped[:])
+    return grouped
 
 
 def tile_gin_pa_kernel(tc, X, A, W_in, b_in, eps0, out):
@@ -51,14 +51,15 @@ def tile_gin_pa_kernel(tc, X, A, W_in, b_in, eps0, out):
         keep = ctx.enter_context(tc.tile_pool(name="keep", bufs=1))
         stage = ctx.enter_context(tc.tile_pool(name="stage", bufs=4))
         psum = ctx.enter_context(tc.psum_pool(name="psum", bufs=8))
+        ctx.enter_context(tc.manual_schedule())
 
         ones = keep.tile([P, P], BF16, name="ones")
         nc.vector.memset(ones[:], 1.0)
         b_row = keep.tile([P, HID], BF16, name="b_row")
         nc.vector.memset(b_row[:], 0.0)
-        nc.sync.dma_start(out=b_row[0:1, :], in_=b_in.rearrange("(o f) -> o f", o=1))
+        nc.scalar.dma_start(out=b_row[0:1, :], in_=b_in.rearrange("(o f) -> o f", o=1))
         eps_bf = keep.tile([P, 1], BF16, name="eps_bf")
-        nc.sync.dma_start(out=eps_bf[:], in_=eps0.partition_broadcast(P))
+        nc.scalar.dma_start(out=eps_bf[:], in_=eps0.partition_broadcast(P))
         x_rows = []
         for c in range(PAIRS):
             x_rows.append(keep.tile([P, 2 * IN_DIM], BF16, name="x_rows%d" % c))
@@ -78,16 +79,17 @@ def tile_gin_pa_kernel(tc, X, A, W_in, b_in, eps0, out):
 
         identity = keep.tile([P, P], F32, name="identity")
         make_identity(nc, identity[:])
-        one_plus_eps = keep.tile([P, 1], F32, name="one_plus_eps")
-        nc.vector.tensor_scalar_add(out=one_plus_eps[:], in0=eps_bf[:], scalar1=1.0)
-        bias_bank = psum.tile([P, HID], F32, tag="bank")
-        nc.tensor.matmul(out=bias_bank[:], lhsT=ones[:], rhs=b_row[:], start=True, stop=True)
-        bias = keep.tile([P, HID], F32, name="bias")
-        nc.scalar.copy(out=bias[:], in_=bias_bank[:])
 
-        w_codes = []
-        w_scales = []
-        for g in range(PASSES):
+        def transposed(rows):
+            return transpose_rows(nc, psum, stage, identity[:], rows[:])
+
+        def quantised(grouped, width, name):
+            codes = keep.tile([P, width], U32, name=name + "_codes", align_bytes=64)
+            scales = keep.tile([P, width], U8, name=name + "_scales", align_bytes=64)
+            nc.vector.quantize_mx(out=codes[:].bitcast(FP8X4), scales=scales[:], in_=grouped[:])
+            return codes, scales
+
+        def regroup_w(g):
             w_grouped = keep.tile([P, 4 * HID], BF16, name="w_grouped%d" % g, align_bytes=64)
             nc.vector.tensor_copy(
                 out=w_grouped[:, : 4 * W_VECTOR_COLS].rearrange("p (c i t) -> p c t i", i=4, t=4),
@@ -97,70 +99,81 @@ def tile_gin_pa_kernel(tc, X, A, W_in, b_in, eps0, out):
                 out=w_grouped[:, 4 * W_VECTOR_COLS :].rearrange("p (c i t) -> p c t i", i=4, t=4),
                 in_=w_raw[g][:, :, W_VECTOR_COLS:].rearrange("p t (c i) -> p c t i", i=4),
             )
-            codes = keep.tile([P, HID], U32, name="w_codes%d" % g, align_bytes=64)
-            scales = keep.tile([P, HID], U8, name="w_scales%d" % g, align_bytes=64)
-            nc.vector.quantize_mx(out=codes[:].bitcast(FP8X4), scales=scales[:], in_=w_grouped[:])
-            w_codes.append(codes)
-            w_scales.append(scales)
+            return w_grouped
 
-        def quantise_rows(rows, name):
-            codes = keep.tile([P, 4 * P], U32, name=name + "_codes", align_bytes=64)
-            scales = keep.tile([P, 4 * P], U8, name=name + "_scales", align_bytes=64)
-            transpose_and_quantise(nc, psum, stage, identity[:], rows[:], codes[:], scales[:])
-            return codes, scales
+        pair_rows = x_rows + a_rows
+        grouped = {}
+        pair_q = {}
 
-        h32 = []
-        h_codes = []
-        h_scales = []
+        def transpose_pair(i):
+            grouped[i] = transposed(pair_rows[i])
 
-        def project(g, x_q):
-            h_f32 = keep.tile([P, 4, HID], F32, name="h32_%d" % g)
-            h_grouped = keep.tile([P, 4 * HID], BF16, name="h_grouped%d" % g, align_bytes=64)
-            codes_h = keep.tile([P, HID], U32, name="h_codes%d" % g, align_bytes=64)
-            scales_h = keep.tile([P, HID], U8, name="h_scales%d" % g, align_bytes=64)
+        def quantise_pair(i):
+            pair_q[i] = quantised(grouped[i], 4 * P, "pair%d" % i)
+
+        transpose_pair(0)
+        w_grouped0 = regroup_w(0)
+        quantise_pair(0)
+        w_grouped1 = regroup_w(1)
+        w_q = [quantised(w_grouped0, HID, "w0"), quantised(w_grouped1, HID, "w1")]
+        transpose_pair(1)
+
+        bias_bank = psum.tile([P, HID], F32, tag="bank")
+        nc.tensor.matmul(out=bias_bank[:], lhsT=ones[:], rhs=b_row[:], start=True, stop=True)
+        bias = keep.tile([P, HID], F32, name="bias")
+        nc.scalar.copy(out=bias[:], in_=bias_bank[:])
+        one_plus_eps = keep.tile([P, 1], F32, name="one_plus_eps")
+        nc.vector.tensor_scalar_add(out=one_plus_eps[:], in0=eps_bf[:], scalar1=1.0)
+
+        quantise_pair(1)
+        transpose_pair(2)
+        transpose_pair(3)
+
+        h32 = [keep.tile([P, 4, HID], F32, name="h32_%d" % g) for g in range(PASSES)]
+        h_grouped = [keep.tile([P, 4 * HID], BF16, name="h_grouped%d" % g, align_bytes=64) for g in range(PASSES)]
+        h_codes = [keep.tile([P, HID], U32, name="h_codes%d" % g, align_bytes=64) for g in range(PASSES)]
+        h_scales = [keep.tile([P, HID], U8, name="h_scales%d" % g, align_bytes=64) for g in range(PASSES)]
+
+        for g in range(PASSES):
             for cf in range(F_CHUNKS):
                 f_cols = slice(cf * P, (cf + 1) * P)
                 bank = psum.tile([P, 4, P], F32, tag="bank")
                 for t in range(4):
-                    codes, scales = x_q[2 * g + t // 2]
+                    codes, scales = pair_q[2 * g + t // 2]
                     for kp in range(PASSES):
                         first = ((t % 2) * PASSES + kp) * P
                         nc.tensor.matmul_mx(
                             out=bank[:, t, :],
                             lhsT=codes[:, first : first + P].bitcast(FP8X4),
                             lhsT_scale=scales[:, first : first + P],
-                            rhs=w_codes[kp][:, f_cols].bitcast(FP8X4),
-                            rhs_scale=w_scales[kp][:, f_cols],
+                            rhs=w_q[kp][0][:, f_cols].bitcast(FP8X4),
+                            rhs_scale=w_q[kp][1][:, f_cols],
                             start=(kp == 0),
                             stop=(kp == PASSES - 1),
                         )
                 nc.vector.tensor_tensor(
-                    out=h_f32[:, :, f_cols],
+                    out=h32[g][:, :, f_cols],
                     in0=bank[:],
                     in1=bias[:, f_cols].unsqueeze(1).to_broadcast([P, 4, P]),
                     op=ADD,
                 )
                 nc.scalar.copy(
-                    out=h_grouped[:, cf * 4 * P : (cf + 1) * 4 * P].rearrange("p (f t) -> p f t", t=4),
-                    in_=h_f32[:, :, f_cols].rearrange("p t f -> p f t"),
+                    out=h_grouped[g][:, cf * 4 * P : (cf + 1) * 4 * P].rearrange("p (f t) -> p f t", t=4),
+                    in_=h32[g][:, :, f_cols].rearrange("p t f -> p f t"),
                 )
+            quantise_pair(2 * g + 2)
+            quantise_pair(2 * g + 3)
+            transpose_pair(2 * g + 4)
+            transpose_pair(2 * g + 5)
+            for cf in range(F_CHUNKS):
                 nc.vector.quantize_mx(
-                    out=codes_h[:, f_cols].bitcast(FP8X4),
-                    scales=scales_h[:, f_cols],
-                    in_=h_grouped[:, cf * 4 * P : (cf + 1) * 4 * P],
+                    out=h_codes[g][:, cf * P : (cf + 1) * P].bitcast(FP8X4),
+                    scales=h_scales[g][:, cf * P : (cf + 1) * P],
+                    in_=h_grouped[g][:, cf * 4 * P : (cf + 1) * 4 * P],
                 )
-            h32.append(h_f32)
-            h_codes.append(codes_h)
-            h_scales.append(scales_h)
-
-        x_q = [quantise_rows(x_rows[c], "x%d" % c) for c in range(PAIRS)]
-        for g in range(PASSES):
-            project(g, x_q)
-
-        a_q = [quantise_rows(a_rows[c], "a%d" % c) for c in range(PAIRS)]
 
         for c in range(PAIRS):
-            codes, scales = a_q[c]
+            codes, scales = pair_q[PAIRS + c]
             for e in range(2):
                 acc = psum.tile([P, HID], F32, tag="bank")
                 for g in range(PASSES):
@@ -184,3 +197,5 @@ def tile_gin_pa_kernel(tc, X, A, W_in, b_in, eps0, out):
                     op1=ADD,
                 )
                 nc.sync.dma_start(out=out_view[c][:, e, :], in_=result[:])
+            if c + 2 < PAIRS:
+                quantise_pair(PAIRS + c + 2)

@@ -158,8 +158,8 @@ def tile_gin_pa_kernel(tc, X, A, W_in, b_in, eps0, out):
                     op=ADD,
                 )
                 nc.scalar.copy(
-                    out=h_grouped[g][:, cf * 4 * P : (cf + 1) * 4 * P].rearrange("p (f t) -> p f t", t=4),
-                    in_=h32[g][:, :, f_cols].rearrange("p t f -> p f t"),
+                    out=h_grouped[g][:, cf * 4 * P : (cf + 1) * 4 * P].rearrange("p (c i t) -> p c t i", i=4, t=4),
+                    in_=h32[g][:, :, f_cols].rearrange("p t (c i) -> p c t i", i=4),
                 )
             quantise_pair(2 * g + 2)
             quantise_pair(2 * g + 3)

@@ -15,29 +15,12 @@ P = 128
 NODES = 1024
 IN_DIM = 1024
 HID = 512
-K_PASS = 4 * P
 PASSES = 2
 PAIRS = NODES // (2 * P)
-F_CHUNKS = HID // P
-W_VECTOR_COLS = 2 * HID // 3 // 8 * 8
+HALVES = 2
+HALF = HID // HALVES
 
 FLOPS = 2 * NODES * IN_DIM * HID + 2 * NODES * NODES * HID
-
-
-def transpose_rows(nc, psum, stage, identity, rows):
-    words = rows.bitcast(F32)
-    grouped = stage.tile([P, 2 * IN_DIM], BF16, tag="grouped", align_bytes=64)
-    grouped_words = grouped[:].bitcast(F32)
-    for e in range(2):
-        bank = psum.tile([P, 4, P], F32, tag="bank")
-        for gu in range(4):
-            first = e * (IN_DIM // 2) + gu * P
-            nc.tensor.transpose(bank[:, gu, :], words[:, first : first + P], identity)
-        nc.scalar.copy(
-            out=grouped_words[:, e * 512 : (e + 1) * 512].rearrange("p (g r u) -> p g r u", g=2, u=2),
-            in_=bank[:].rearrange("p (g u) r -> p g r u", u=2),
-        )
-    return grouped
 
 
 def tile_gin_pa_kernel(tc, X, A, W_in, b_in, eps0, out):
@@ -49,153 +32,268 @@ def tile_gin_pa_kernel(tc, X, A, W_in, b_in, eps0, out):
 
     with ExitStack() as ctx:
         keep = ctx.enter_context(tc.tile_pool(name="keep", bufs=1))
-        stage = ctx.enter_context(tc.tile_pool(name="stage", bufs=4))
         psum = ctx.enter_context(tc.psum_pool(name="psum", bufs=8))
         ctx.enter_context(tc.manual_schedule())
 
-        ones = keep.tile([P, P], BF16, name="ones")
-        nc.vector.memset(ones[:], 1.0)
         b_row = keep.tile([P, HID], BF16, name="b_row")
         nc.vector.memset(b_row[:], 0.0)
-        nc.scalar.dma_start(out=b_row[0:1, :], in_=b_in.rearrange("(o f) -> o f", o=1))
+        ones = keep.tile([P, P], BF16, name="ones")
+        nc.vector.memset(ones[:], 1.0)
         eps_bf = keep.tile([P, 1], BF16, name="eps_bf")
-        nc.scalar.dma_start(out=eps_bf[:], in_=eps0.partition_broadcast(P))
-        x_rows = []
-        for c in range(PAIRS):
-            x_rows.append(keep.tile([P, 2 * IN_DIM], BF16, name="x_rows%d" % c))
-        nc.sync.dma_start(out=x_rows[0][:], in_=x_view[0])
-        w_raw = []
-        for g in range(PASSES):
-            w_rows = keep.tile([P, 4, HID], BF16, name="w_raw%d" % g)
-            nc.sync.dma_start(out=w_rows[:].rearrange("p (u e) f -> p u (e f)", u=2), in_=w_view[g])
-            w_raw.append(w_rows)
-        for c in range(1, PAIRS):
-            nc.sync.dma_start(out=x_rows[c][:], in_=x_view[c])
-        a_rows = []
-        for c in range(PAIRS):
-            rows = keep.tile([P, 2 * NODES], BF16, name="a_rows%d" % c)
-            nc.sync.dma_start(out=rows[:], in_=a_view[c])
-            a_rows.append(rows)
+
+        def load_b():
+            nc.sync.dma_start(out=b_row[0:1, :], in_=b_in.rearrange("(o f) -> o f", o=1))
+
+        def load_eps():
+            nc.sync.dma_start(out=eps_bf[:], in_=eps0.partition_broadcast(P))
+
+        rows = []
+        for i in range(2 * PAIRS):
+            rows.append(keep.tile([P, 2 * IN_DIM], BF16, name="rows%d" % i))
+        w_raw = [keep.tile([P, 4, HID], BF16, name="w_raw%d" % g) for g in range(PASSES)]
+
+        def load_w(g):
+            nc.sync.dma_start(out=w_raw[g][:].rearrange("p (u e) f -> p u (e f)", u=2), in_=w_view[g])
+
+        def load_rows(i, e=None):
+            source = x_view[i] if i < PAIRS else a_view[i - PAIRS]
+            cols = slice(0, 2 * IN_DIM) if e is None else slice(e * IN_DIM, (e + 1) * IN_DIM)
+            nc.sync.dma_start(out=rows[i][:, cols], in_=source[:, cols])
+
+        load_w(0)
+        load_b()
+        load_rows(0, 0)
+        load_rows(0, 1)
+        load_w(1)
+        load_rows(1)
+        load_eps()
+        load_rows(2)
+        load_rows(3)
+        load_rows(4)
+        load_rows(5)
+        load_rows(6)
+        load_rows(7)
 
         identity = keep.tile([P, P], F32, name="identity")
         make_identity(nc, identity[:])
 
-        def transposed(rows):
-            return transpose_rows(nc, psum, stage, identity[:], rows[:])
+        grouped = []
+        pair_codes = []
+        pair_scales = []
+        for i in range(2 * PAIRS):
+            grouped.append(keep.tile([P, 2 * IN_DIM], BF16, name="grouped%d" % i, align_bytes=64))
+            pair_codes.append(keep.tile([P, 4 * P], U32, name="pair_codes%d" % i, align_bytes=64))
+            pair_scales.append(keep.tile([P, 4 * P], U8, name="pair_scales%d" % i, align_bytes=64))
+        banks = {}
 
-        def quantised(grouped, width, name):
-            codes = keep.tile([P, width], U32, name=name + "_codes", align_bytes=64)
-            scales = keep.tile([P, width], U8, name=name + "_scales", align_bytes=64)
-            nc.vector.quantize_mx(out=codes[:].bitcast(FP8X4), scales=scales[:], in_=grouped[:])
-            return codes, scales
+        def transpose(i):
+            words = rows[i][:].bitcast(F32)
+            for e in range(2):
+                bank = psum.tile([P, 4, P], F32, tag="bank")
+                for gu in range(4):
+                    first = e * (IN_DIM // 2) + gu * P
+                    nc.tensor.transpose(bank[:, gu, :], words[:, first : first + P], identity[:])
+                banks["t", i, e] = bank
 
-        def regroup_w(g):
-            w_grouped = keep.tile([P, 4 * HID], BF16, name="w_grouped%d" % g, align_bytes=64)
-            nc.vector.tensor_copy(
-                out=w_grouped[:, : 4 * W_VECTOR_COLS].rearrange("p (c i t) -> p c t i", i=4, t=4),
-                in_=w_raw[g][:, :, :W_VECTOR_COLS].rearrange("p t (c i) -> p c t i", i=4),
+        def empty(i, e, engine="s"):
+            copy = nc.scalar.copy if engine == "s" else nc.vector.tensor_copy
+            copy(
+                out=grouped[i][:].bitcast(F32)[:, e * 512 : (e + 1) * 512].rearrange("p (g r u) -> p g r u", g=2, u=2),
+                in_=banks["t", i, e][:].rearrange("p (g u) r -> p g r u", u=2),
             )
-            nc.scalar.copy(
-                out=w_grouped[:, 4 * W_VECTOR_COLS :].rearrange("p (c i t) -> p c t i", i=4, t=4),
-                in_=w_raw[g][:, :, W_VECTOR_COLS:].rearrange("p t (c i) -> p c t i", i=4),
+
+        def quantise(i):
+            nc.vector.quantize_mx(out=pair_codes[i][:].bitcast(FP8X4), scales=pair_scales[i][:], in_=grouped[i][:])
+
+        w_grouped = {}
+        w_codes = {}
+        w_scales = {}
+        h_grouped = {}
+        h_codes = {}
+        h_scales = {}
+        for half in range(HALVES):
+            for g in range(PASSES):
+                key = "%d%d" % (half, g)
+                w_grouped[half, g] = keep.tile([P, 4 * HALF], BF16, name="w_grouped" + key, align_bytes=64)
+                w_codes[half, g] = keep.tile([P, HALF], U32, name="w_codes" + key, align_bytes=64)
+                w_scales[half, g] = keep.tile([P, HALF], U8, name="w_scales" + key, align_bytes=64)
+                h_grouped[half, g] = keep.tile([P, 4 * HALF], BF16, name="h_grouped" + key, align_bytes=64)
+                h_codes[half, g] = keep.tile([P, HALF], U32, name="h_codes" + key, align_bytes=64)
+                h_scales[half, g] = keep.tile([P, HALF], U8, name="h_scales" + key, align_bytes=64)
+        h32 = [keep.tile([P, 4, HID], F32, name="h32_%d" % g) for g in range(PASSES)]
+
+        def cols(half):
+            return slice(half * HALF, (half + 1) * HALF)
+
+        def regroup_w(half, g, engine):
+            copy = nc.scalar.copy if engine == "s" else nc.vector.tensor_copy
+            copy(
+                out=w_grouped[half, g][:].rearrange("p (c i t) -> p c t i", i=4, t=4),
+                in_=w_raw[g][:, :, cols(half)].rearrange("p t (c i) -> p c t i", i=4),
             )
-            return w_grouped
 
-        pair_rows = x_rows + a_rows
-        grouped = {}
-        pair_q = {}
+        def quantise_w(half, g):
+            nc.vector.quantize_mx(
+                out=w_codes[half, g][:].bitcast(FP8X4), scales=w_scales[half, g][:], in_=w_grouped[half, g][:]
+            )
 
-        def transpose_pair(i):
-            grouped[i] = transposed(pair_rows[i])
+        def product(half, i):
+            bank = psum.tile([P, 2, HALF], F32, tag="bank")
+            for e in range(2):
+                for kp in range(PASSES):
+                    first = (e * PASSES + kp) * P
+                    nc.tensor.matmul_mx(
+                        out=bank[:, e, :],
+                        lhsT=pair_codes[i][:, first : first + P].bitcast(FP8X4),
+                        lhsT_scale=pair_scales[i][:, first : first + P],
+                        rhs=w_codes[half, kp][:].bitcast(FP8X4),
+                        rhs_scale=w_scales[half, kp][:],
+                        start=(kp == 0),
+                        stop=(kp == PASSES - 1),
+                    )
+            banks["h", half, i] = bank
 
-        def quantise_pair(i):
-            pair_q[i] = quantised(grouped[i], 4 * P, "pair%d" % i)
+        def h_rows(half, i):
+            return h32[i // 2][:, 2 * (i % 2) : 2 * (i % 2) + 2, cols(half)]
 
-        transpose_pair(0)
-        w_grouped0 = regroup_w(0)
-        quantise_pair(0)
-        w_grouped1 = regroup_w(1)
-        w_q = [quantised(w_grouped0, HID, "w0"), quantised(w_grouped1, HID, "w1")]
-        transpose_pair(1)
+        def add_bias(half, i):
+            nc.vector.tensor_tensor(
+                out=h_rows(half, i),
+                in0=banks["h", half, i][:],
+                in1=bias[:, cols(half)].unsqueeze(1).to_broadcast([P, 2, HALF]),
+                op=ADD,
+            )
+
+        def cast(half, g):
+            for part in range(2):
+                first = half * HALF + part * P
+                nc.scalar.copy(
+                    out=h_grouped[half, g][:, part * 4 * P : (part + 1) * 4 * P].rearrange(
+                        "p (c i t) -> p c t i", i=4, t=4
+                    ),
+                    in_=h32[g][:, :, first : first + P].rearrange("p t (c i) -> p c t i", i=4),
+                )
+
+        def quantise_h(half, g):
+            nc.vector.quantize_mx(
+                out=h_codes[half, g][:].bitcast(FP8X4), scales=h_scales[half, g][:], in_=h_grouped[half, g][:]
+            )
+
+        def aggregate(half, c):
+            bank = psum.tile([P, 2, HALF], F32, tag="bank")
+            for e in range(2):
+                for g in range(PASSES):
+                    first = (e * PASSES + g) * P
+                    nc.tensor.matmul_mx(
+                        out=bank[:, e, :],
+                        lhsT=pair_codes[PAIRS + c][:, first : first + P].bitcast(FP8X4),
+                        lhsT_scale=pair_scales[PAIRS + c][:, first : first + P],
+                        rhs=h_codes[half, g][:].bitcast(FP8X4),
+                        rhs_scale=h_scales[half, g][:],
+                        start=(g == 0),
+                        stop=(g == PASSES - 1),
+                    )
+            banks["o", half, c] = bank
+
+        def finish(half, c):
+            result = keep.tile([P, 2, HALF], F32, name="result%d%d" % (half, c))
+            nc.vector.scalar_tensor_tensor(
+                out=result[:],
+                in0=h_rows(half, c),
+                scalar=one_plus_eps[:, 0:1],
+                in1=banks["o", half, c][:],
+                op0=MULT,
+                op1=ADD,
+            )
+            nc.sync.dma_start(out=out_view[c][:, :, cols(half)], in_=result[:])
 
         bias_bank = psum.tile([P, HID], F32, tag="bank")
         nc.tensor.matmul(out=bias_bank[:], lhsT=ones[:], rhs=b_row[:], start=True, stop=True)
         bias = keep.tile([P, HID], F32, name="bias")
         nc.scalar.copy(out=bias[:], in_=bias_bank[:])
         one_plus_eps = keep.tile([P, 1], F32, name="one_plus_eps")
-        nc.vector.tensor_scalar_add(out=one_plus_eps[:], in0=eps_bf[:], scalar1=1.0)
 
-        quantise_pair(1)
-        transpose_pair(2)
-        transpose_pair(3)
+        def add_one():
+            nc.vector.tensor_scalar_add(out=one_plus_eps[:], in0=eps_bf[:], scalar1=1.0)
 
-        h32 = [keep.tile([P, 4, HID], F32, name="h32_%d" % g) for g in range(PASSES)]
-        h_grouped = [keep.tile([P, 4 * HID], BF16, name="h_grouped%d" % g, align_bytes=64) for g in range(PASSES)]
-        h_codes = [keep.tile([P, HID], U32, name="h_codes%d" % g, align_bytes=64) for g in range(PASSES)]
-        h_scales = [keep.tile([P, HID], U8, name="h_scales%d" % g, align_bytes=64) for g in range(PASSES)]
-
-        for g in range(PASSES):
-            for cf in range(F_CHUNKS):
-                f_cols = slice(cf * P, (cf + 1) * P)
-                bank = psum.tile([P, 4, P], F32, tag="bank")
-                for t in range(4):
-                    codes, scales = pair_q[2 * g + t // 2]
-                    for kp in range(PASSES):
-                        first = ((t % 2) * PASSES + kp) * P
-                        nc.tensor.matmul_mx(
-                            out=bank[:, t, :],
-                            lhsT=codes[:, first : first + P].bitcast(FP8X4),
-                            lhsT_scale=scales[:, first : first + P],
-                            rhs=w_q[kp][0][:, f_cols].bitcast(FP8X4),
-                            rhs_scale=w_q[kp][1][:, f_cols],
-                            start=(kp == 0),
-                            stop=(kp == PASSES - 1),
-                        )
-                nc.vector.tensor_tensor(
-                    out=h32[g][:, :, f_cols],
-                    in0=bank[:],
-                    in1=bias[:, f_cols].unsqueeze(1).to_broadcast([P, 4, P]),
-                    op=ADD,
-                )
-                nc.scalar.copy(
-                    out=h_grouped[g][:, cf * 4 * P : (cf + 1) * 4 * P].rearrange("p (c i t) -> p c t i", i=4, t=4),
-                    in_=h32[g][:, :, f_cols].rearrange("p t (c i) -> p c t i", i=4),
-                )
-            quantise_pair(2 * g + 2)
-            quantise_pair(2 * g + 3)
-            transpose_pair(2 * g + 4)
-            transpose_pair(2 * g + 5)
-            for cf in range(F_CHUNKS):
-                nc.vector.quantize_mx(
-                    out=h_codes[g][:, cf * P : (cf + 1) * P].bitcast(FP8X4),
-                    scales=h_scales[g][:, cf * P : (cf + 1) * P],
-                    in_=h_grouped[g][:, cf * 4 * P : (cf + 1) * 4 * P],
-                )
-
-        for c in range(PAIRS):
-            codes, scales = pair_q[PAIRS + c]
-            for e in range(2):
-                acc = psum.tile([P, HID], F32, tag="bank")
-                for g in range(PASSES):
-                    first = (e * PASSES + g) * P
-                    nc.tensor.matmul_mx(
-                        out=acc[:],
-                        lhsT=codes[:, first : first + P].bitcast(FP8X4),
-                        lhsT_scale=scales[:, first : first + P],
-                        rhs=h_codes[g][:].bitcast(FP8X4),
-                        rhs_scale=h_scales[g][:],
-                        start=(g == 0),
-                        stop=(g == PASSES - 1),
-                    )
-                result = stage.tile([P, HID], F32, tag="result")
-                nc.vector.scalar_tensor_tensor(
-                    out=result[:],
-                    in0=h32[c // 2][:, 2 * (c % 2) + e, :],
-                    scalar=one_plus_eps[:, 0:1],
-                    in1=acc[:],
-                    op0=MULT,
-                    op1=ADD,
-                )
-                nc.sync.dma_start(out=out_view[c][:, e, :], in_=result[:])
-            if c + 2 < PAIRS:
-                quantise_pair(PAIRS + c + 2)
+        regroup_w(0, 0, "v")
+        regroup_w(1, 0, "v")
+        quantise_w(0, 0)
+        quantise_w(1, 0)
+        transpose(0)
+        empty(0, 0)
+        empty(0, 1)
+        regroup_w(0, 1, "v")
+        regroup_w(1, 1, "s")
+        quantise_w(0, 1)
+        transpose(1)
+        quantise(0)
+        product(0, 0)
+        empty(1, 0)
+        empty(1, 1)
+        transpose(2)
+        quantise_w(1, 1)
+        add_bias(0, 0)
+        quantise(1)
+        empty(2, 0)
+        empty(2, 1)
+        transpose(3)
+        product(1, 0)
+        product(0, 1)
+        add_bias(1, 0)
+        quantise(2)
+        empty(3, 0)
+        empty(3, 1)
+        transpose(4)
+        add_bias(0, 1)
+        add_one()
+        product(1, 1)
+        product(0, 2)
+        quantise(3)
+        empty(4, 0)
+        empty(4, 1)
+        add_bias(1, 1)
+        product(0, 3)
+        cast(0, 0)
+        add_bias(0, 2)
+        product(1, 2)
+        product(1, 3)
+        cast(1, 0)
+        transpose(5)
+        add_bias(0, 3)
+        quantise_h(0, 0)
+        empty(5, 0)
+        empty(5, 1)
+        add_bias(1, 2)
+        add_bias(1, 3)
+        quantise(4)
+        cast(0, 1)
+        quantise_h(1, 0)
+        transpose(6)
+        quantise(5)
+        empty(6, 0)
+        empty(6, 1)
+        quantise_h(0, 1)
+        transpose(7)
+        cast(1, 1)
+        aggregate(0, 0)
+        aggregate(0, 1)
+        empty(7, 0)
+        empty(7, 1)
+        quantise(6)
+        finish(0, 0)
+        finish(0, 1)
+        aggregate(0, 2)
+        quantise_h(1, 1)
+        aggregate(1, 0)
+        finish(0, 2)
+        quantise(7)
+        aggregate(0, 3)
+        finish(1, 0)
+        aggregate(1, 1)
+        finish(0, 3)
+        aggregate(1, 2)
+        finish(1, 1)
+        finish(1, 2)
+        aggregate(1, 3)
+        finish(1, 3)

@@ -234,66 +234,66 @@ def tile_gin_pa_kernel(tc, X, A, W_in, b_in, eps0, out):
         transpose(2)
         quantise_w(1, 1)
         add_bias(0, 0)
+        add_one()
         quantise(1)
         empty(2, 0)
         empty(2, 1)
         transpose(3)
-        product(1, 0)
         product(0, 1)
-        add_bias(1, 0)
-        quantise(2)
-        empty(3, 0)
+        empty(3, 0, "v")
         empty(3, 1)
+        quantise(2)
         transpose(4)
         add_bias(0, 1)
-        add_one()
+        product(1, 0)
         product(1, 1)
         product(0, 2)
         quantise(3)
         empty(4, 0)
         empty(4, 1)
+        add_bias(1, 0)
         add_bias(1, 1)
         product(0, 3)
         cast(0, 0)
         add_bias(0, 2)
+        add_bias(0, 3)
         product(1, 2)
         product(1, 3)
         cast(1, 0)
         transpose(5)
-        add_bias(0, 3)
         quantise_h(0, 0)
-        empty(5, 0)
-        empty(5, 1)
+        quantise(4)
         add_bias(1, 2)
         add_bias(1, 3)
-        quantise(4)
         cast(0, 1)
+        empty(5, 0)
+        empty(5, 1)
         quantise_h(1, 0)
         transpose(6)
-        quantise(5)
-        empty(6, 0)
-        empty(6, 1)
         quantise_h(0, 1)
-        transpose(7)
+        quantise(5)
         cast(1, 1)
+        transpose(7)
         aggregate(0, 0)
         aggregate(0, 1)
+        finish(0, 0)
+        empty(6, 0)
+        empty(6, 1)
+        quantise_h(1, 1)
+        finish(0, 1)
+        aggregate(1, 0)
+        quantise(6)
+        aggregate(1, 1)
+        finish(1, 0)
         empty(7, 0)
         empty(7, 1)
-        quantise(6)
-        finish(0, 0)
-        finish(0, 1)
-        aggregate(0, 2)
-        quantise_h(1, 1)
-        aggregate(1, 0)
-        finish(0, 2)
-        quantise(7)
-        aggregate(0, 3)
-        finish(1, 0)
-        aggregate(1, 1)
-        finish(0, 3)
-        aggregate(1, 2)
         finish(1, 1)
+        aggregate(0, 2)
+        quantise(7)
+        finish(0, 2)
+        aggregate(1, 2)
+        aggregate(0, 3)
         finish(1, 2)
+        finish(0, 3)
         aggregate(1, 3)
         finish(1, 3)

@@ -65,14 +65,17 @@ def tile_gin_pa_kernel(tc, X, A, W_in, b_in, eps0, out):
         load_rows(0, 0)
         load_rows(0, 1)
         load_w(1)
-        load_rows(1)
-        load_eps()
-        load_rows(2)
-        load_rows(3)
+        load_rows(1, 0)
+        load_rows(1, 1)
+        load_rows(2, 0)
+        load_rows(2, 1)
+        load_rows(3, 0)
+        load_rows(3, 1)
         load_rows(4)
         load_rows(5)
         load_rows(6)
         load_rows(7)
+        load_eps()
 
         identity = keep.tile([P, P], F32, name="identity")
         make_identity(nc, identity[:])
@@ -102,8 +105,13 @@ def tile_gin_pa_kernel(tc, X, A, W_in, b_in, eps0, out):
                 in_=banks["t", i, e][:].rearrange("p (g u) r -> p g r u", u=2),
             )
 
-        def quantise(i):
-            nc.vector.quantize_mx(out=pair_codes[i][:].bitcast(FP8X4), scales=pair_scales[i][:], in_=grouped[i][:])
+        def quantise(i, e=None):
+            words = slice(0, 4 * P) if e is None else slice(e * 2 * P, (e + 1) * 2 * P)
+            nc.vector.quantize_mx(
+                out=pair_codes[i][:, words].bitcast(FP8X4),
+                scales=pair_scales[i][:, words],
+                in_=grouped[i][:, 4 * words.start : 4 * words.stop],
+            )
 
         w_grouped = {}
         w_codes = {}
@@ -207,6 +215,14 @@ def tile_gin_pa_kernel(tc, X, A, W_in, b_in, eps0, out):
             )
             nc.sync.dma_start(out=out_view[c][:, :, cols(half)], in_=result[:])
 
+        warm_bank = psum.tile([P, P], F32, tag="bank")
+
+        def keep_busy(count):
+            for repeat in range(count):
+                nc.tensor.matmul(out=warm_bank[:], lhsT=ones[:], rhs=ones[:], start=True, stop=True)
+
+        keep_busy(16)
+
         bias_bank = psum.tile([P, HID], F32, tag="bank")
         nc.tensor.matmul(out=bias_bank[:], lhsT=ones[:], rhs=b_row[:], start=True, stop=True)
         bias = keep.tile([P, HID], F32, name="bias")
@@ -214,33 +230,34 @@ def tile_gin_pa_kernel(tc, X, A, W_in, b_in, eps0, out):
         one_plus_eps = keep.tile([P, 1], F32, name="one_plus_eps")
 
         def add_one():
-            nc.vector.tensor_scalar_add(out=one_plus_eps[:], in0=eps_bf[:], scalar1=1.0)
+            nc.gpsimd.tensor_scalar(out=one_plus_eps[:], in0=eps_bf[:], scalar1=1.0, scalar2=None, op0=ADD)
 
         regroup_w(0, 0, "v")
-        regroup_w(1, 0, "v")
-        quantise_w(0, 0)
-        quantise_w(1, 0)
         transpose(0)
+        keep_busy(8)
         empty(0, 0)
         empty(0, 1)
+        regroup_w(1, 0, "v")
+        quantise_w(0, 0)
+        quantise(0, 0)
         regroup_w(0, 1, "v")
+        quantise(0, 1)
         regroup_w(1, 1, "s")
         quantise_w(0, 1)
         transpose(1)
-        quantise(0)
         product(0, 0)
+        quantise_w(1, 0)
+        quantise_w(1, 1)
         empty(1, 0)
         empty(1, 1)
         transpose(2)
-        quantise_w(1, 1)
         add_bias(0, 0)
-        add_one()
         quantise(1)
         empty(2, 0)
         empty(2, 1)
         transpose(3)
-        product(0, 1)
         empty(3, 0, "v")
+        product(0, 1)
         empty(3, 1)
         quantise(2)
         transpose(4)
@@ -276,6 +293,7 @@ def tile_gin_pa_kernel(tc, X, A, W_in, b_in, eps0, out):
         transpose(7)
         aggregate(0, 0)
         aggregate(0, 1)
+        add_one()
         finish(0, 0)
         empty(6, 0)
         empty(6, 1)

@@ -67,8 +67,7 @@ def tile_gin_pa_kernel(tc, X, A, W_in, b_in, eps0, out):
         load_w(1)
         load_rows(1, 0)
         load_rows(1, 1)
-        load_rows(2, 0)
-        load_rows(2, 1)
+        load_rows(2)
         load_rows(3, 0)
         load_rows(3, 1)
         load_rows(4)
@@ -237,27 +236,27 @@ def tile_gin_pa_kernel(tc, X, A, W_in, b_in, eps0, out):
         keep_busy(8)
         empty(0, 0)
         empty(0, 1)
-        regroup_w(1, 0, "v")
         quantise_w(0, 0)
-        quantise(0, 0)
+        regroup_w(1, 0, "v")
         regroup_w(0, 1, "v")
-        quantise(0, 1)
+        quantise(0, 0)
         regroup_w(1, 1, "s")
         quantise_w(0, 1)
+        quantise(0, 1)
         transpose(1)
         product(0, 0)
-        quantise_w(1, 0)
-        quantise_w(1, 1)
         empty(1, 0)
         empty(1, 1)
+        quantise_w(1, 0)
+        quantise_w(1, 1)
         transpose(2)
         add_bias(0, 0)
         quantise(1)
         empty(2, 0)
         empty(2, 1)
         transpose(3)
-        empty(3, 0, "v")
         product(0, 1)
+        empty(3, 0)
         empty(3, 1)
         quantise(2)
         transpose(4)
@@ -279,15 +278,15 @@ def tile_gin_pa_kernel(tc, X, A, W_in, b_in, eps0, out):
         cast(1, 0)
         transpose(5)
         quantise_h(0, 0)
-        quantise(4)
         add_bias(1, 2)
+        quantise(4)
         add_bias(1, 3)
         cast(0, 1)
         empty(5, 0)
         empty(5, 1)
-        quantise_h(1, 0)
         transpose(6)
         quantise_h(0, 1)
+        quantise_h(1, 0)
         quantise(5)
         cast(1, 1)
         transpose(7)
@@ -305,13 +304,13 @@ def tile_gin_pa_kernel(tc, X, A, W_in, b_in, eps0, out):
         finish(1, 0)
         empty(7, 0)
         empty(7, 1)
+        quantise(7)
         finish(1, 1)
         aggregate(0, 2)
-        quantise(7)
         finish(0, 2)
         aggregate(1, 2)
         aggregate(0, 3)
         finish(1, 2)
-        finish(0, 3)
         aggregate(1, 3)
+        finish(0, 3)
         finish(1, 3)

@@ -88,9 +88,9 @@ def tile_gin_pa_kernel(tc, X, A, W_in, b_in, eps0, out):
             pair_scales.append(keep.tile([P, 4 * P], U8, name="pair_scales%d" % i, align_bytes=64))
         banks = {}
 
-        def transpose(i):
+        def transpose(i, tiles=(0, 1)):
             words = rows[i][:].bitcast(F32)
-            for e in range(2):
+            for e in tiles:
                 bank = psum.tile([P, 4, P], F32, tag="bank")
                 for gu in range(4):
                     first = e * (IN_DIM // 2) + gu * P
@@ -233,7 +233,7 @@ def tile_gin_pa_kernel(tc, X, A, W_in, b_in, eps0, out):
 
         regroup_w(0, 0, "v")
         transpose(0)
-        keep_busy(8)
+        keep_busy(12)
         empty(0, 0)
         empty(0, 1)
         quantise_w(0, 0)
@@ -243,7 +243,9 @@ def tile_gin_pa_kernel(tc, X, A, W_in, b_in, eps0, out):
         regroup_w(1, 1, "s")
         quantise_w(0, 1)
         quantise(0, 1)
-        transpose(1)
+        transpose(1, (0,))
+        keep_busy(3)
+        transpose(1, (1,))
         product(0, 0)
         empty(1, 0)
         empty(1, 1)

from contextlib import ExitStack

import concourse.mybir as mybir
from concourse.masks import make_identity

F32 = mybir.dt.float32
BF16 = mybir.dt.bfloat16
U32 = mybir.dt.uint32
U8 = mybir.dt.uint8
FP8X4 = mybir.dt.float8_e4m3fn_x4
ADD = mybir.AluOpType.add
MULT = mybir.AluOpType.mult

P = 128
NODES = 1024
IN_DIM = 1024
HID = 512
PASSES = 2
PAIRS = NODES // (2 * P)
HALVES = 2
HALF = HID // HALVES

FLOPS = 2 * NODES * IN_DIM * HID + 2 * NODES * NODES * HID


def tile_gin_pa_kernel(tc, X, A, W_in, b_in, eps0, out):
    nc = tc.nc
    x_view = X.rearrange("(c p e) k -> c p (e k)", p=P, e=2)
    a_view = A.rearrange("(c p e) m -> c p (e m)", p=P, e=2)
    out_view = out.rearrange("(c p e) f -> c p e f", p=P, e=2)
    w_view = W_in.rearrange("(g u p e) f -> g p u (e f)", g=PASSES, u=2, p=P)

    with ExitStack() as ctx:
        keep = ctx.enter_context(tc.tile_pool(name="keep", bufs=1))
        psum = ctx.enter_context(tc.psum_pool(name="psum", bufs=8))
        ctx.enter_context(tc.manual_schedule())

        b_row = keep.tile([P, HID], BF16, name="b_row")
        nc.vector.memset(b_row[:], 0.0)
        ones = keep.tile([P, P], BF16, name="ones")
        nc.vector.memset(ones[:], 1.0)
        eps_bf = keep.tile([P, 1], BF16, name="eps_bf")

        def load_b():
            nc.sync.dma_start(out=b_row[0:1, :], in_=b_in.rearrange("(o f) -> o f", o=1))

        def load_eps():
            nc.sync.dma_start(out=eps_bf[:], in_=eps0.partition_broadcast(P))

        rows = []
        for i in range(2 * PAIRS):
            rows.append(keep.tile([P, 2 * IN_DIM], BF16, name="rows%d" % i))
        w_raw = [keep.tile([P, 4, HID], BF16, name="w_raw%d" % g) for g in range(PASSES)]

        def load_w(g):
            nc.sync.dma_start(out=w_raw[g][:].rearrange("p (u e) f -> p u (e f)", u=2), in_=w_view[g])

        def load_rows(i, e=None):
            source = x_view[i] if i < PAIRS else a_view[i - PAIRS]
            cols = slice(0, 2 * IN_DIM) if e is None else slice(e * IN_DIM, (e + 1) * IN_DIM)
            nc.sync.dma_start(out=rows[i][:, cols], in_=source[:, cols])

        load_w(0)
        load_b()
        load_rows(0, 0)
        load_rows(0, 1)
        load_w(1)
        load_rows(1, 0)
        load_rows(1, 1)
        load_rows(2)
        load_rows(3, 0)
        load_rows(3, 1)
        load_rows(4)
        load_rows(5)
        load_rows(6)
        load_rows(7)
        load_eps()

        identity = keep.tile([P, P], F32, name="identity")
        make_identity(nc, identity[:])

        grouped = []
        pair_codes = []
        pair_scales = []
        for i in range(2 * PAIRS):
            grouped.append(keep.tile([P, 2 * IN_DIM], BF16, name="grouped%d" % i, align_bytes=64))
            pair_codes.append(keep.tile([P, 4 * P], U32, name="pair_codes%d" % i, align_bytes=64))
            pair_scales.append(keep.tile([P, 4 * P], U8, name="pair_scales%d" % i, align_bytes=64))
        banks = {}

        def transpose(i, tiles=(0, 1)):
            words = rows[i][:].bitcast(F32)
            for e in tiles:
                bank = psum.tile([P, 4, P], F32, tag="bank")
                for gu in range(4):
                    first = e * (IN_DIM // 2) + gu * P
                    nc.tensor.transpose(bank[:, gu, :], words[:, first : first + P], identity[:])
                banks["t", i, e] = bank

        def empty(i, e, engine="s"):
            copy = nc.scalar.copy if engine == "s" else nc.vector.tensor_copy
            copy(
                out=grouped[i][:].bitcast(F32)[:, e * 512 : (e + 1) * 512].rearrange("p (g r u) -> p g r u", g=2, u=2),
                in_=banks["t", i, e][:].rearrange("p (g u) r -> p g r u", u=2),
            )

        def quantise(i, e=None):
            words = slice(0, 4 * P) if e is None else slice(e * 2 * P, (e + 1) * 2 * P)
            nc.vector.quantize_mx(
                out=pair_codes[i][:, words].bitcast(FP8X4),
                scales=pair_scales[i][:, words],
                in_=grouped[i][:, 4 * words.start : 4 * words.stop],
            )

        w_grouped = {}
        w_codes = {}
        w_scales = {}
        h_grouped = {}
        h_codes = {}
        h_scales = {}
        for half in range(HALVES):
            for g in range(PASSES):
                key = "%d%d" % (half, g)
                w_grouped[half, g] = keep.tile([P, 4 * HALF], BF16, name="w_grouped" + key, align_bytes=64)
                w_codes[half, g] = keep.tile([P, HALF], U32, name="w_codes" + key, align_bytes=64)
                w_scales[half, g] = keep.tile([P, HALF], U8, name="w_scales" + key, align_bytes=64)
                h_grouped[half, g] = keep.tile([P, 4 * HALF], BF16, name="h_grouped" + key, align_bytes=64)
                h_codes[half, g] = keep.tile([P, HALF], U32, name="h_codes" + key, align_bytes=64)
                h_scales[half, g] = keep.tile([P, HALF], U8, name="h_scales" + key, align_bytes=64)
        h32 = [keep.tile([P, 4, HID], F32, name="h32_%d" % g) for g in range(PASSES)]

        def cols(half):
            return slice(half * HALF, (half + 1) * HALF)

        def regroup_w(half, g, engine):
            copy = nc.scalar.copy if engine == "s" else nc.vector.tensor_copy
            copy(
                out=w_grouped[half, g][:].rearrange("p (c i t) -> p c t i", i=4, t=4),
                in_=w_raw[g][:, :, cols(half)].rearrange("p t (c i) -> p c t i", i=4),
            )

        def quantise_w(half, g):
            nc.vector.quantize_mx(
                out=w_codes[half, g][:].bitcast(FP8X4), scales=w_scales[half, g][:], in_=w_grouped[half, g][:]
            )

        def product(half, i):
            bank = psum.tile([P, 2, HALF], F32, tag="bank")
            for e in range(2):
                for kp in range(PASSES):
                    first = (e * PASSES + kp) * P
                    nc.tensor.matmul_mx(
                        out=bank[:, e, :],
                        lhsT=pair_codes[i][:, first : first + P].bitcast(FP8X4),
                        lhsT_scale=pair_scales[i][:, first : first + P],
                        rhs=w_codes[half, kp][:].bitcast(FP8X4),
                        rhs_scale=w_scales[half, kp][:],
                        start=(kp == 0),
                        stop=(kp == PASSES - 1),
                    )
            banks["h", half, i] = bank

        def h_rows(half, i):
            return h32[i // 2][:, 2 * (i % 2) : 2 * (i % 2) + 2, cols(half)]

        def add_bias(half, i):
            nc.vector.tensor_tensor(
                out=h_rows(half, i),
                in0=banks["h", half, i][:],
                in1=bias[:, cols(half)].unsqueeze(1).to_broadcast([P, 2, HALF]),
                op=ADD,
            )

        def cast(half, g):
            for part in range(2):
                first = half * HALF + part * P
                nc.scalar.copy(
                    out=h_grouped[half, g][:, part * 4 * P : (part + 1) * 4 * P].rearrange(
                        "p (c i t) -> p c t i", i=4, t=4
                    ),
                    in_=h32[g][:, :, first : first + P].rearrange("p t (c i) -> p c t i", i=4),
                )

        def quantise_h(half, g):
            nc.vector.quantize_mx(
                out=h_codes[half, g][:].bitcast(FP8X4), scales=h_scales[half, g][:], in_=h_grouped[half, g][:]
            )

        def aggregate(half, c):
            bank = psum.tile([P, 2, HALF], F32, tag="bank")
            for e in range(2):
                for g in range(PASSES):
                    first = (e * PASSES + g) * P
                    nc.tensor.matmul_mx(
                        out=bank[:, e, :],
                        lhsT=pair_codes[PAIRS + c][:, first : first + P].bitcast(FP8X4),
                        lhsT_scale=pair_scales[PAIRS + c][:, first : first + P],
                        rhs=h_codes[half, g][:].bitcast(FP8X4),
                        rhs_scale=h_scales[half, g][:],
                        start=(g == 0),
                        stop=(g == PASSES - 1),
                    )
            banks["o", half, c] = bank

        def finish(half, c):
            result = keep.tile([P, 2, HALF], F32, name="result%d%d" % (half, c))
            nc.vector.scalar_tensor_tensor(
                out=result[:],
                in0=h_rows(half, c),
                scalar=one_plus_eps[:, 0:1],
                in1=banks["o", half, c][:],
                op0=MULT,
                op1=ADD,
            )
            nc.sync.dma_start(out=out_view[c][:, :, cols(half)], in_=result[:])

        warm_bank = psum.tile([P, P], F32, tag="bank")

        def keep_busy(count):
            for repeat in range(count):
                nc.tensor.matmul(out=warm_bank[:], lhsT=ones[:], rhs=ones[:], start=True, stop=True)

        keep_busy(16)

        bias_bank = psum.tile([P, HID], F32, tag="bank")
        nc.tensor.matmul(out=bias_bank[:], lhsT=ones[:], rhs=b_row[:], start=True, stop=True)
        bias = keep.tile([P, HID], F32, name="bias")
        nc.scalar.copy(out=bias[:], in_=bias_bank[:])
        one_plus_eps = keep.tile([P, 1], F32, name="one_plus_eps")

        def add_one():
            nc.gpsimd.tensor_scalar(out=one_plus_eps[:], in0=eps_bf[:], scalar1=1.0, scalar2=None, op0=ADD)

        regroup_w(0, 0, "v")
        transpose(0)
        keep_busy(12)
        empty(0, 0)
        empty(0, 1)
        quantise_w(0, 0)
        regroup_w(1, 0, "v")
        regroup_w(0, 1, "v")
        quantise(0, 0)
        regroup_w(1, 1, "s")
        quantise_w(0, 1)
        quantise(0, 1)
        transpose(1, (0,))
        keep_busy(3)
        transpose(1, (1,))
        product(0, 0)
        empty(1, 0)
        empty(1, 1)
        quantise_w(1, 0)
        quantise_w(1, 1)
        transpose(2)
        add_bias(0, 0)
        quantise(1)
        empty(2, 0)
        empty(2, 1)
        transpose(3)
        product(0, 1)
        empty(3, 0)
        empty(3, 1)
        quantise(2)
        transpose(4)
        add_bias(0, 1)
        product(1, 0)
        product(1, 1)
        product(0, 2)
        quantise(3)
        empty(4, 0)
        empty(4, 1)
        add_bias(1, 0)
        add_bias(1, 1)
        product(0, 3)
        cast(0, 0)
        add_bias(0, 2)
        add_bias(0, 3)
        product(1, 2)
        product(1, 3)
        cast(1, 0)
        transpose(5)
        quantise_h(0, 0)
        add_bias(1, 2)
        quantise(4)
        add_bias(1, 3)
        cast(0, 1)
        empty(5, 0)
        empty(5, 1)
        transpose(6)
        quantise_h(0, 1)
        quantise_h(1, 0)
        quantise(5)
        cast(1, 1)
        transpose(7)
        aggregate(0, 0)
        aggregate(0, 1)
        add_one()
        finish(0, 0)
        empty(6, 0)
        empty(6, 1)
        quantise_h(1, 1)
        finish(0, 1)
        aggregate(1, 0)
        quantise(6)
        aggregate(1, 1)
        finish(1, 0)
        empty(7, 0)
        empty(7, 1)
        quantise(7)
        finish(1, 1)
        aggregate(0, 2)
        finish(0, 2)
        aggregate(1, 2)
        aggregate(0, 3)
        finish(1, 2)
        aggregate(1, 3)
        finish(0, 3)
        finish(1, 3)
